import numpy as np
import ml_dtypes

BF16 = ml_dtypes.bfloat16


def bf(x):
    return np.asarray(x, np.float32).astype(BF16)


def f32(x):
    return np.asarray(x, np.float32)


def f64(x):
    return np.asarray(x).astype(np.float64)


def striped(idx):
    return np.tile(idx.reshape(-1, 16).T, (8, 1))


C, F, S, N = 512, 2048, 2048, 512
EPS = 1e-6
ERF_LIMIT, ERF_TERMS = 6.0, 150


def erf(a):
    c = np.clip(a, -ERF_LIMIT, ERF_LIMIT)
    term = c.copy()
    total = c.copy()
    for n in range(1, ERF_TERMS):
        term = term * (2.0 * c * c / (2 * n + 1))
        total = total + term
    r = 2.0 / np.sqrt(np.pi) * np.exp(-c * c) * total
    return np.where(np.abs(a) > ERF_LIMIT, np.sign(a), r)


def gelu_erf(v):
    return 0.5 * v * (1.0 + erf(v / np.sqrt(2.0)))


def setup_inputs():
    return {"base": f32(np.random.standard_normal((C, S))), "x": f32(np.random.standard_normal((C, N))), "norm_w": f32(1.0 + 0.1 * np.random.standard_normal((C, 1))), "w1": bf(np.random.standard_normal((C, F)) / np.sqrt(C)), "w2": bf(np.random.standard_normal((F, C)) / np.sqrt(F)), "offs": striped(np.random.permutation(S)[:N])}


def reference(base, x, norm_w, w1, w2, offs):
    idx = offs[:16].T.reshape(-1)
    xs = f64(x)
    h = xs / np.sqrt(np.mean(xs * xs, axis=0, keepdims=True) + EPS) * f64(norm_w)
    u = gelu_erf(f64(w1).T @ h)
    y = f64(w2).T @ u
    out = f64(base).copy()
    out[:, idx] = xs + y
    return out

@@ -1,0 +1,113 @@
+from contextlib import ExitStack
+
+import concourse.mybir as mybir
+
+F32 = mybir.dt.float32
+BF16 = mybir.dt.bfloat16
+U16 = mybir.dt.uint16
+ACT = mybir.ActivationFunctionType
+ALU = mybir.AluOpType
+
+P = 128
+C, F, S, N = 512, 2048, 2048, 512
+CB = C // P
+FB = F // P
+FQ = 4
+FB_PER_Q = FB // FQ
+EPS = 1e-6
+
+FLOPS = 2 * C * F * N * 2
+
+
+def tile_synthetictransformer_kernel(tc, base, x, norm_w, w1, w2, offs, out):
+    nc = tc.nc
+    with ExitStack() as ctx:
+        held = ctx.enter_context(tc.tile_pool(name="held", bufs=1))
+        ring = ctx.enter_context(tc.tile_pool(name="ring", bufs=2))
+        psum_norm = ctx.enter_context(tc.psum_pool(name="psum_norm", bufs=1))
+        psum_u = ctx.enter_context(tc.psum_pool(name="psum_u", bufs=4))
+        psum_y = ctx.enter_context(tc.psum_pool(name="psum_y", bufs=2))
+
+        queues = (nc.sync, nc.scalar)
+
+        x_sb = [held.tile([P, N], F32, name=f"x{cb}") for cb in range(CB)]
+        for cb in range(CB):
+            queues[cb % 2].dma_start(x_sb[cb][:], x[cb * P : (cb + 1) * P, :])
+
+        gain_row = held.tile([1, C], F32, name="gain_row")
+        nc.scalar.dma_start(gain_row[:], norm_w.rearrange("c o -> o c"))
+
+        offsets = held.tile([P, N // 16], U16, name="offsets")
+        nc.sync.dma_start(offsets[:], offs)
+
+        w1_sb = [held.tile([P, CB, F // FQ], BF16, name=f"w1_{q}") for q in range(FQ)]
+        for q in range(FQ):
+            queues[q % 2].dma_start(
+                w1_sb[q][:],
+                w1[:, q * (F // FQ) : (q + 1) * (F // FQ)].rearrange("(cb p) f -> p cb f", p=P),
+            )
+
+        w2_sb = [held.tile([P, FB // 2, C], BF16, name=f"w2_{half}") for half in range(2)]
+        for half in range(2):
+            queues[half].dma_start(
+                w2_sb[half][:],
+                w2[half * (F // 2) : (half + 1) * (F // 2), :].rearrange("(fb p) c -> p fb c", p=P),
+            )
+
+        window = [held.tile([P, S], F32, name=f"window{cb}") for cb in range(CB)]
+        for cb in range(CB):
+            queues[cb % 2].dma_start(window[cb][:], base[cb * P : (cb + 1) * P, :])
+
+        averager = held.tile([P, P], F32, name="averager")
+        nc.vector.memset(averager[:], 1.0 / C)
+        eps = held.tile([P, 1], F32, name="eps")
+        nc.vector.memset(eps[:], EPS)
+        unit = held.tile([1, 1], F32, name="unit")
+        nc.vector.memset(unit[:], 1.0)
+
+        gain_ps = psum_norm.tile([P, CB], F32, name="gain_ps")
+        for cb in range(CB):
+            nc.tensor.matmul(
+                gain_ps[:, cb : cb + 1], gain_row[:, cb * P : (cb + 1) * P], unit[:], start=True, stop=True
+            )
+        gain = held.tile([P, CB], F32, name="gain")
+        nc.vector.tensor_copy(gain[:], gain_ps[:])
+
+        mean_ps = psum_norm.tile([P, N], F32, name="mean_ps")
+        for cb in range(CB):
+            squares = held.tile([P, N], F32, name=f"squares{cb}")
+            nc.vector.tensor_tensor(squares[:], x_sb[cb][:], x_sb[cb][:], ALU.mult)
+            nc.tensor.matmul(mean_ps[:], averager[:], squares[:], start=(cb == 0), stop=(cb == CB - 1))
+        r = held.tile([P, N], F32, name="r")
+        nc.scalar.activation(r[:], mean_ps[:], ACT.Abs_reciprocal_sqrt, bias=eps[:], scale=1.0)
+
+        h = [held.tile([P, N], BF16, name=f"h{cb}") for cb in range(CB)]
+        for cb in range(CB):
+            nc.vector.scalar_tensor_tensor(
+                h[cb][:], x_sb[cb][:], gain[:, cb : cb + 1], r[:], ALU.mult, ALU.mult
+            )
+
+        u = [held.tile([P, N], BF16, name=f"u{fb}") for fb in range(FB)]
+        for fb in range(FB):
+            q, f0 = fb // FB_PER_Q, (fb % FB_PER_Q) * P
+            u_ps = psum_u.tile([P, N], F32, name="u_ps")
+            for cb in range(CB):
+                nc.tensor.matmul(
+                    u_ps[:], w1_sb[q][:, cb, f0 : f0 + P], h[cb][:], start=(cb == 0), stop=(cb == CB - 1)
+                )
+            nc.scalar.activation(u[fb][:], u_ps[:], ACT.Gelu)
+
+        for cb in range(CB):
+            y_ps = psum_y.tile([P, N], F32, name="y_ps")
+            for fb in range(FB):
+                nc.tensor.matmul(
+                    y_ps[:],
+                    w2_sb[fb // (FB // 2)][:, fb % (FB // 2), cb * P : (cb + 1) * P],
+                    u[fb][:],
+                    start=(fb == 0),
+                    stop=(fb == FB - 1),
+                )
+            y = ring.tile([P, N], F32, name="y")
+            nc.scalar.copy(y[:], y_ps[:])
+            nc.vector.tensor_tensor(window[cb][:].indirect(offsets[:]), y[:], x_sb[cb][:], ALU.add)
+            nc.sync.dma_start(out[cb * P : (cb + 1) * P, :], window[cb][:])

@@ -15,6 +15,9 @@ FB = F // P
 FQ = 4
 FB_PER_Q = FB // FQ
 EPS = 1e-6
+HALVES = 2
+NH = N // HALVES
+GROUP = 2
 
 FLOPS = 2 * C * F * N * 2
 
@@ -24,79 +27,84 @@ def tile_synthetictransformer_kernel(tc, base, x, norm_w, w1, w2, offs, out):
     with ExitStack() as ctx:
         held = ctx.enter_context(tc.tile_pool(name="held", bufs=1))
         ring = ctx.enter_context(tc.tile_pool(name="ring", bufs=2))
-        psum_norm = ctx.enter_context(tc.psum_pool(name="psum_norm", bufs=1))
-        psum_u = ctx.enter_context(tc.psum_pool(name="psum_u", bufs=4))
-        psum_y = ctx.enter_context(tc.psum_pool(name="psum_y", bufs=2))
+        psum_u = ctx.enter_context(tc.psum_pool(name="psum_u", bufs=6))
+        halves = [slice(half * NH, (half + 1) * NH) for half in range(HALVES)]
 
-        queues = (nc.sync, nc.scalar)
+        x_sb = held.tile([P, CB, N], F32, name="x_sb")
+        x_blocks = x.rearrange("(cb p) j -> p cb j", p=P)
+        for cols in halves:
+            nc.sync.dma_start(x_sb[:, 0:2, cols], x_blocks[:, 0:2, cols])
+            nc.scalar.dma_start(x_sb[:, 2:4, cols], x_blocks[:, 2:4, cols])
 
-        x_sb = [held.tile([P, N], F32, name=f"x{cb}") for cb in range(CB)]
-        for cb in range(CB):
-            queues[cb % 2].dma_start(x_sb[cb][:], x[cb * P : (cb + 1) * P, :])
-
-        gain_row = held.tile([1, C], F32, name="gain_row")
-        nc.scalar.dma_start(gain_row[:], norm_w.rearrange("c o -> o c"))
-
-        offsets = held.tile([P, N // 16], U16, name="offsets")
-        nc.sync.dma_start(offsets[:], offs)
+        gain = held.tile([P, CB], F32, name="gain")
+        with nc.allow_non_contiguous_dma(reason="512 single values, needed only for h"):
+            nc.sync.dma_start(gain[:], norm_w.rearrange("(cb p) o -> p (cb o)", p=P))
 
         w1_sb = [held.tile([P, CB, F // FQ], BF16, name=f"w1_{q}") for q in range(FQ)]
         for q in range(FQ):
-            queues[q % 2].dma_start(
+            (nc.sync, nc.scalar)[q % 2].dma_start(
                 w1_sb[q][:],
                 w1[:, q * (F // FQ) : (q + 1) * (F // FQ)].rearrange("(cb p) f -> p cb f", p=P),
             )
 
-        w2_sb = [held.tile([P, FB // 2, C], BF16, name=f"w2_{half}") for half in range(2)]
-        for half in range(2):
-            queues[half].dma_start(
-                w2_sb[half][:],
-                w2[half * (F // 2) : (half + 1) * (F // 2), :].rearrange("(fb p) c -> p fb c", p=P),
+        offsets = held.tile([P, N // 16], U16, name="offsets")
+        nc.sync.dma_start(offsets[:], offs)
+
+        w2_sb = [held.tile([P, FB // 2, C], BF16, name=f"w2_{part}") for part in range(2)]
+        for part in range(2):
+            nc.sync.dma_start(
+                w2_sb[part][:],
+                w2[part * (F // 2) : (part + 1) * (F // 2), :].rearrange("(fb p) c -> p fb c", p=P),
             )
 
         window = [held.tile([P, S], F32, name=f"window{cb}") for cb in range(CB)]
         for cb in range(CB):
-            queues[cb % 2].dma_start(window[cb][:], base[cb * P : (cb + 1) * P, :])
+            nc.sync.dma_start(window[cb][:], base[cb * P : (cb + 1) * P, :])
 
         averager = held.tile([P, P], F32, name="averager")
         nc.vector.memset(averager[:], 1.0 / C)
         eps = held.tile([P, 1], F32, name="eps")
         nc.vector.memset(eps[:], EPS)
-        unit = held.tile([1, 1], F32, name="unit")
-        nc.vector.memset(unit[:], 1.0)
 
-        gain_ps = psum_norm.tile([P, CB], F32, name="gain_ps")
-        for cb in range(CB):
-            nc.tensor.matmul(
-                gain_ps[:, cb : cb + 1], gain_row[:, cb * P : (cb + 1) * P], unit[:], start=True, stop=True
-            )
-        gain = held.tile([P, CB], F32, name="gain")
-        nc.vector.tensor_copy(gain[:], gain_ps[:])
-
-        mean_ps = psum_norm.tile([P, N], F32, name="mean_ps")
-        for cb in range(CB):
-            squares = held.tile([P, N], F32, name=f"squares{cb}")
-            nc.vector.tensor_tensor(squares[:], x_sb[cb][:], x_sb[cb][:], ALU.mult)
-            nc.tensor.matmul(mean_ps[:], averager[:], squares[:], start=(cb == 0), stop=(cb == CB - 1))
         r = held.tile([P, N], F32, name="r")
-        nc.scalar.activation(r[:], mean_ps[:], ACT.Abs_reciprocal_sqrt, bias=eps[:], scale=1.0)
+        with tc.psum_pool(name="psum_norm", bufs=1) as psum_norm:
+            for half, cols in enumerate(halves):
+                squares = held.tile([P, CB, NH], F32, name=f"squares{half}")
+                nc.scalar.activation(squares[:, 0:2, :], x_sb[:, 0:2, cols], ACT.Square)
+                nc.vector.tensor_tensor(squares[:, 2:4, :], x_sb[:, 2:4, cols], x_sb[:, 2:4, cols], ALU.mult)
+                pairs = held.tile([P, 2, NH], F32, name=f"pairs{half}")
+                nc.vector.tensor_tensor(pairs[:], squares[:, 0:2, :], squares[:, 2:4, :], ALU.add)
+                mean_ps = psum_norm.tile([P, NH], F32, name=f"mean_ps{half}")
+                for k in range(2):
+                    nc.tensor.matmul(mean_ps[:], averager[:], pairs[:, k, :], start=(k == 0), stop=(k == 1))
+                nc.scalar.activation(r[:, cols], mean_ps[:], ACT.Abs_reciprocal_sqrt, bias=eps[:], scale=1.0)
 
-        h = [held.tile([P, N], BF16, name=f"h{cb}") for cb in range(CB)]
-        for cb in range(CB):
-            nc.vector.scalar_tensor_tensor(
-                h[cb][:], x_sb[cb][:], gain[:, cb : cb + 1], r[:], ALU.mult, ALU.mult
-            )
+        h = held.tile([P, CB, N], BF16, name="h")
+        for cols in halves:
+            for cb in range(CB):
+                nc.vector.scalar_tensor_tensor(
+                    h[:, cb, cols], x_sb[:, cb, cols], gain[:, cb : cb + 1], r[:, cols], ALU.mult, ALU.mult
+                )
 
         u = [held.tile([P, N], BF16, name=f"u{fb}") for fb in range(FB)]
-        for fb in range(FB):
-            q, f0 = fb // FB_PER_Q, (fb % FB_PER_Q) * P
-            u_ps = psum_u.tile([P, N], F32, name="u_ps")
-            for cb in range(CB):
-                nc.tensor.matmul(
-                    u_ps[:], w1_sb[q][:, cb, f0 : f0 + P], h[cb][:], start=(cb == 0), stop=(cb == CB - 1)
-                )
-            nc.scalar.activation(u[fb][:], u_ps[:], ACT.Gelu)
+        for cols in halves:
+            for first in range(0, FB, GROUP):
+                group = range(first, first + GROUP)
+                u_ps = {fb: psum_u.tile([P, NH], F32, name="u_ps") for fb in group}
+                for cb in range(CB):
+                    for fb in group:
+                        q, f0 = fb // FB_PER_Q, (fb % FB_PER_Q) * P
+                        nc.tensor.matmul(
+                            u_ps[fb][:],
+                            w1_sb[q][:, cb, f0 : f0 + P],
+                            h[:, cb, cols],
+                            start=(cb == 0),
+                            stop=(cb == CB - 1),
+                        )
+                for fb in group:
+                    nc.scalar.activation(u[fb][:, cols], u_ps[fb][:], ACT.Gelu)
 
+        psum_y = ctx.enter_context(tc.psum_pool(name="psum_y", bufs=2))
         for cb in range(CB):
             y_ps = psum_y.tile([P, N], F32, name="y_ps")
             for fb in range(FB):
@@ -109,5 +117,5 @@ def tile_synthetictransformer_kernel(tc, base, x, norm_w, w1, w2, offs, out):
                 )
             y = ring.tile([P, N], F32, name="y")
             nc.scalar.copy(y[:], y_ps[:])
-            nc.vector.tensor_tensor(window[cb][:].indirect(offsets[:]), y[:], x_sb[cb][:], ALU.add)
+            nc.vector.tensor_tensor(window[cb][:].indirect(offsets[:]), y[:], x_sb[:, cb, :], ALU.add)
             nc.sync.dma_start(out[cb * P : (cb + 1) * P, :], window[cb][:])

@@ -18,6 +18,7 @@ EPS = 1e-6
 HALVES = 2
 NH = N // HALVES
 GROUP = 2
+WARM_UP = 9
 
 FLOPS = 2 * C * F * N * 2
 
@@ -27,7 +28,7 @@ def tile_synthetictransformer_kernel(tc, base, x, norm_w, w1, w2, offs, out):
     with ExitStack() as ctx:
         held = ctx.enter_context(tc.tile_pool(name="held", bufs=1))
         ring = ctx.enter_context(tc.tile_pool(name="ring", bufs=2))
-        psum_u = ctx.enter_context(tc.psum_pool(name="psum_u", bufs=6))
+        psum_u = ctx.enter_context(tc.psum_pool(name="psum_u", bufs=5))
         halves = [slice(half * NH, (half + 1) * NH) for half in range(HALVES)]
 
         x_sb = held.tile([P, CB, N], F32, name="x_sb")
@@ -61,6 +62,8 @@ def tile_synthetictransformer_kernel(tc, base, x, norm_w, w1, w2, offs, out):
         for cb in range(CB):
             nc.sync.dma_start(window[cb][:], base[cb * P : (cb + 1) * P, :])
 
+        zeros = held.tile([P, N], BF16, name="zeros")
+        nc.vector.memset(zeros[:], 0.0)
         averager = held.tile([P, P], F32, name="averager")
         nc.vector.memset(averager[:], 1.0 / C)
         eps = held.tile([P, 1], F32, name="eps")
@@ -68,6 +71,10 @@ def tile_synthetictransformer_kernel(tc, base, x, norm_w, w1, w2, offs, out):
 
         r = held.tile([P, N], F32, name="r")
         with tc.psum_pool(name="psum_norm", bufs=1) as psum_norm:
+            idle_ps = psum_norm.tile([P, N], F32, name="idle_ps")
+            for i in range(WARM_UP):
+                nc.tensor.matmul(idle_ps[:], zeros[:, 0:P], zeros[:], start=True, stop=True)
+
             for half, cols in enumerate(halves):
                 squares = held.tile([P, CB, NH], F32, name=f"squares{half}")
                 nc.scalar.activation(squares[:, 0:2, :], x_sb[:, 0:2, cols], ACT.Square)

@@ -69,6 +69,9 @@ def tile_synthetictransformer_kernel(tc, base, x, norm_w, w1, w2, offs, out):
         eps = held.tile([P, 1], F32, name="eps")
         nc.vector.memset(eps[:], EPS)
 
+        first_call = held.tile([P, 1], F32, name="first_call")
+        nc.scalar.activation(first_call[:], eps[:], ACT.Abs_reciprocal_sqrt)
+
         r = held.tile([P, N], F32, name="r")
         with tc.psum_pool(name="psum_norm", bufs=1) as psum_norm:
             idle_ps = psum_norm.tile([P, N], F32, name="idle_ps")
@@ -77,12 +80,13 @@ def tile_synthetictransformer_kernel(tc, base, x, norm_w, w1, w2, offs, out):
 
             for half, cols in enumerate(halves):
                 squares = held.tile([P, CB, NH], F32, name=f"squares{half}")
-                nc.scalar.activation(squares[:, 0:2, :], x_sb[:, 0:2, cols], ACT.Square)
-                nc.vector.tensor_tensor(squares[:, 2:4, :], x_sb[:, 2:4, cols], x_sb[:, 2:4, cols], ALU.mult)
+                for k in range(2):
+                    nc.scalar.activation(squares[:, k, :], x_sb[:, k, cols], ACT.Square)
+                    nc.vector.tensor_tensor(squares[:, k + 2, :], x_sb[:, k + 2, cols], x_sb[:, k + 2, cols], ALU.mult)
                 pairs = held.tile([P, 2, NH], F32, name=f"pairs{half}")
-                nc.vector.tensor_tensor(pairs[:], squares[:, 0:2, :], squares[:, 2:4, :], ALU.add)
                 mean_ps = psum_norm.tile([P, NH], F32, name=f"mean_ps{half}")
                 for k in range(2):
+                    nc.vector.tensor_tensor(pairs[:, k, :], squares[:, k, :], squares[:, k + 2, :], ALU.add)
                     nc.tensor.matmul(mean_ps[:], averager[:], pairs[:, k, :], start=(k == 0), stop=(k == 1))
                 nc.scalar.activation(r[:, cols], mean_ps[:], ACT.Abs_reciprocal_sqrt, bias=eps[:], scale=1.0)
 

@@ -12,13 +12,13 @@ P = 128
 C, F, S, N = 512, 2048, 2048, 512
 CB = C // P
 FB = F // P
-FQ = 4
-FB_PER_Q = FB // FQ
 EPS = 1e-6
 HALVES = 2
 NH = N // HALVES
-GROUP = 2
-WARM_UP = 9
+PAIR = 2
+FQ = FB // PAIR
+FW = F // FQ
+WARM_UP = 4
 
 FLOPS = 2 * C * F * N * 2
 
@@ -28,25 +28,24 @@ def tile_synthetictransformer_kernel(tc, base, x, norm_w, w1, w2, offs, out):
     with ExitStack() as ctx:
         held = ctx.enter_context(tc.tile_pool(name="held", bufs=1))
         ring = ctx.enter_context(tc.tile_pool(name="ring", bufs=2))
+        scaled_ring = ctx.enter_context(tc.tile_pool(name="scaled_ring", bufs=8))
         psum_u = ctx.enter_context(tc.psum_pool(name="psum_u", bufs=5))
         halves = [slice(half * NH, (half + 1) * NH) for half in range(HALVES)]
 
-        x_sb = held.tile([P, CB, N], F32, name="x_sb")
-        x_blocks = x.rearrange("(cb p) j -> p cb j", p=P)
-        for cols in halves:
-            nc.sync.dma_start(x_sb[:, 0:2, cols], x_blocks[:, 0:2, cols])
-            nc.scalar.dma_start(x_sb[:, 2:4, cols], x_blocks[:, 2:4, cols])
-
         gain = held.tile([P, CB], F32, name="gain")
-        with nc.allow_non_contiguous_dma(reason="512 single values, needed only for h"):
+        with nc.allow_non_contiguous_dma(reason="512 single values"):
             nc.sync.dma_start(gain[:], norm_w.rearrange("(cb p) o -> p (cb o)", p=P))
 
-        w1_sb = [held.tile([P, CB, F // FQ], BF16, name=f"w1_{q}") for q in range(FQ)]
-        for q in range(FQ):
-            (nc.sync, nc.scalar)[q % 2].dma_start(
-                w1_sb[q][:],
-                w1[:, q * (F // FQ) : (q + 1) * (F // FQ)].rearrange("(cb p) f -> p cb f", p=P),
-            )
+        x_sb = held.tile([P, CB, N], F32, name="x_sb")
+        x_blocks = x.rearrange("(cb p) j -> p cb j", p=P)
+        w1_sb = [held.tile([P, CB, FW], BF16, name=f"w1_{q}") for q in range(FQ)]
+        w1_pieces = [w1[:, q * FW : (q + 1) * FW].rearrange("(cb p) f -> p cb f", p=P) for q in range(FQ)]
+        for half, cols in enumerate(halves):
+            nc.sync.dma_start(x_sb[:, 0:2, cols], x_blocks[:, 0:2, cols])
+            nc.scalar.dma_start(x_sb[:, 2:4, cols], x_blocks[:, 2:4, cols])
+            nc.sync.dma_start(w1_sb[half][:], w1_pieces[half])
+        for q in range(HALVES, FQ):
+            nc.sync.dma_start(w1_sb[q][:], w1_pieces[q])
 
         offsets = held.tile([P, N // 16], U16, name="offsets")
         nc.sync.dma_start(offsets[:], offs)
@@ -72,57 +71,51 @@ def tile_synthetictransformer_kernel(tc, base, x, norm_w, w1, w2, offs, out):
         first_call = held.tile([P, 1], F32, name="first_call")
         nc.scalar.activation(first_call[:], eps[:], ACT.Abs_reciprocal_sqrt)
 
+        psum_norm = ctx.enter_context(tc.psum_pool(name="psum_norm", bufs=1))
+        idle_ps = psum_norm.tile([P, N], F32, name="idle_ps")
+        for i in range(WARM_UP):
+            nc.tensor.matmul(idle_ps[:], zeros[:, 0:P], zeros[:], start=True, stop=True)
+
+        xg = held.tile([P, CB, N], BF16, name="xg")
         r = held.tile([P, N], F32, name="r")
-        with tc.psum_pool(name="psum_norm", bufs=1) as psum_norm:
-            idle_ps = psum_norm.tile([P, N], F32, name="idle_ps")
-            for i in range(WARM_UP):
-                nc.tensor.matmul(idle_ps[:], zeros[:, 0:P], zeros[:], start=True, stop=True)
-
-            for half, cols in enumerate(halves):
-                squares = held.tile([P, CB, NH], F32, name=f"squares{half}")
-                for k in range(2):
-                    nc.scalar.activation(squares[:, k, :], x_sb[:, k, cols], ACT.Square)
-                    nc.vector.tensor_tensor(squares[:, k + 2, :], x_sb[:, k + 2, cols], x_sb[:, k + 2, cols], ALU.mult)
-                pairs = held.tile([P, 2, NH], F32, name=f"pairs{half}")
-                mean_ps = psum_norm.tile([P, NH], F32, name=f"mean_ps{half}")
-                for k in range(2):
-                    nc.vector.tensor_tensor(pairs[:, k, :], squares[:, k, :], squares[:, k + 2, :], ALU.add)
-                    nc.tensor.matmul(mean_ps[:], averager[:], pairs[:, k, :], start=(k == 0), stop=(k == 1))
-                nc.scalar.activation(r[:, cols], mean_ps[:], ACT.Abs_reciprocal_sqrt, bias=eps[:], scale=1.0)
-
-        h = held.tile([P, CB, N], BF16, name="h")
-        for cols in halves:
+        for half, cols in enumerate(halves):
             for cb in range(CB):
-                nc.vector.scalar_tensor_tensor(
-                    h[:, cb, cols], x_sb[:, cb, cols], gain[:, cb : cb + 1], r[:, cols], ALU.mult, ALU.mult
-                )
+                nc.vector.tensor_scalar_mul(xg[:, cb, cols], x_sb[:, cb, cols], gain[:, cb : cb + 1])
+            squares = held.tile([P, CB, NH], F32, name=f"squares{half}")
+            nc.scalar.activation(squares[:], x_sb[:, :, cols], ACT.Square)
+            pairs = held.tile([P, 2, NH], F32, name=f"pairs{half}")
+            nc.vector.tensor_tensor(pairs[:], squares[:, 0:2, :], squares[:, 2:4, :], ALU.add)
+            total = held.tile([P, NH], F32, name=f"total{half}")
+            nc.vector.tensor_tensor(total[:], pairs[:, 0, :], pairs[:, 1, :], ALU.add)
+            mean_ps = psum_norm.tile([P, NH], F32, name=f"mean_ps{half}")
+            nc.tensor.matmul(mean_ps[:], averager[:], total[:], start=True, stop=True)
+            nc.scalar.activation(r[:, cols], mean_ps[:], ACT.Abs_reciprocal_sqrt, bias=eps[:], scale=1.0)
 
-        u = [held.tile([P, N], BF16, name=f"u{fb}") for fb in range(FB)]
+        u = held.tile([P, FB, N], BF16, name="u")
         for cols in halves:
-            for first in range(0, FB, GROUP):
-                group = range(first, first + GROUP)
-                u_ps = {fb: psum_u.tile([P, NH], F32, name="u_ps") for fb in group}
-                for cb in range(CB):
-                    for fb in group:
-                        q, f0 = fb // FB_PER_Q, (fb % FB_PER_Q) * P
+            r_for_pair = r[:, cols].unsqueeze(1).to_broadcast([P, PAIR, NH])
+            for q in range(FQ):
+                u_ps = psum_u.tile([P, PAIR, NH], F32, name="u_ps")
+                for i in range(PAIR):
+                    for cb in range(CB):
                         nc.tensor.matmul(
-                            u_ps[fb][:],
-                            w1_sb[q][:, cb, f0 : f0 + P],
-                            h[:, cb, cols],
+                            u_ps[:, i, :],
+                            w1_sb[q][:, cb, i * P : (i + 1) * P],
+                            xg[:, cb, cols],
                             start=(cb == 0),
                             stop=(cb == CB - 1),
                         )
-                for fb in group:
-                    nc.scalar.activation(u[fb][:, cols], u_ps[fb][:], ACT.Gelu)
+                scaled = scaled_ring.tile([P, PAIR, NH], F32, name="scaled")
+                nc.vector.tensor_tensor(scaled[:], u_ps[:], r_for_pair, ALU.mult)
+                nc.scalar.activation(u[:, q * PAIR : (q + 1) * PAIR, cols], scaled[:], ACT.Gelu)
 
-        psum_y = ctx.enter_context(tc.psum_pool(name="psum_y", bufs=2))
         for cb in range(CB):
-            y_ps = psum_y.tile([P, N], F32, name="y_ps")
+            y_ps = psum_u.tile([P, N], F32, name="y_ps", tag="u_ps")
             for fb in range(FB):
                 nc.tensor.matmul(
                     y_ps[:],
                     w2_sb[fb // (FB // 2)][:, fb % (FB // 2), cb * P : (cb + 1) * P],
-                    u[fb][:],
+                    u[:, fb, :],
                     start=(fb == 0),
                     stop=(fb == FB - 1),
                 )

@@ -13,8 +13,6 @@ C, F, S, N = 512, 2048, 2048, 512
 CB = C // P
 FB = F // P
 EPS = 1e-6
-HALVES = 2
-NH = N // HALVES
 PAIR = 2
 FQ = FB // PAIR
 FW = F // FQ
@@ -29,22 +27,21 @@ def tile_synthetictransformer_kernel(tc, base, x, norm_w, w1, w2, offs, out):
         held = ctx.enter_context(tc.tile_pool(name="held", bufs=1))
         ring = ctx.enter_context(tc.tile_pool(name="ring", bufs=2))
         scaled_ring = ctx.enter_context(tc.tile_pool(name="scaled_ring", bufs=8))
-        psum_u = ctx.enter_context(tc.psum_pool(name="psum_u", bufs=5))
-        halves = [slice(half * NH, (half + 1) * NH) for half in range(HALVES)]
+        psum_sums = ctx.enter_context(tc.psum_pool(name="psum_sums", bufs=6))
+        psum_norm = ctx.enter_context(tc.psum_pool(name="psum_norm", bufs=1))
 
-        gain = held.tile([P, CB], F32, name="gain")
-        with nc.allow_non_contiguous_dma(reason="512 single values"):
-            nc.sync.dma_start(gain[:], norm_w.rearrange("(cb p) o -> p (cb o)", p=P))
-
-        x_sb = held.tile([P, CB, N], F32, name="x_sb")
-        x_blocks = x.rearrange("(cb p) j -> p cb j", p=P)
+        x_sb = [held.tile([P, N], F32, name=f"x{cb}") for cb in range(CB)]
         w1_sb = [held.tile([P, CB, FW], BF16, name=f"w1_{q}") for q in range(FQ)]
         w1_pieces = [w1[:, q * FW : (q + 1) * FW].rearrange("(cb p) f -> p cb f", p=P) for q in range(FQ)]
-        for half, cols in enumerate(halves):
-            nc.sync.dma_start(x_sb[:, 0:2, cols], x_blocks[:, 0:2, cols])
-            nc.scalar.dma_start(x_sb[:, 2:4, cols], x_blocks[:, 2:4, cols])
-            nc.sync.dma_start(w1_sb[half][:], w1_pieces[half])
-        for q in range(HALVES, FQ):
+        gain = held.tile([P, CB], F32, name="gain")
+        with nc.allow_non_contiguous_dma(reason="512 single values"):
+            nc.scalar.dma_start(gain[:], norm_w.rearrange("(cb p) o -> p (cb o)", p=P))
+        nc.sync.dma_start(x_sb[0][:], x[0:P, :])
+        nc.sync.dma_start(w1_sb[0][:], w1_pieces[0])
+        nc.scalar.dma_start(x_sb[1][:], x[P : 2 * P, :])
+        nc.sync.dma_start(x_sb[2][:], x[2 * P : 3 * P, :])
+        nc.scalar.dma_start(x_sb[3][:], x[3 * P : 4 * P, :])
+        for q in range(1, FQ):
             nc.sync.dma_start(w1_sb[q][:], w1_pieces[q])
 
         offsets = held.tile([P, N // 16], U16, name="offsets")
@@ -71,55 +68,55 @@ def tile_synthetictransformer_kernel(tc, base, x, norm_w, w1, w2, offs, out):
         first_call = held.tile([P, 1], F32, name="first_call")
         nc.scalar.activation(first_call[:], eps[:], ACT.Abs_reciprocal_sqrt)
 
-        psum_norm = ctx.enter_context(tc.psum_pool(name="psum_norm", bufs=1))
         idle_ps = psum_norm.tile([P, N], F32, name="idle_ps")
         for i in range(WARM_UP):
             nc.tensor.matmul(idle_ps[:], zeros[:, 0:P], zeros[:], start=True, stop=True)
 
-        xg = held.tile([P, CB, N], BF16, name="xg")
-        r = held.tile([P, N], F32, name="r")
-        for half, cols in enumerate(halves):
-            for cb in range(CB):
-                nc.vector.tensor_scalar_mul(xg[:, cb, cols], x_sb[:, cb, cols], gain[:, cb : cb + 1])
-            squares = held.tile([P, CB, NH], F32, name=f"squares{half}")
-            nc.scalar.activation(squares[:], x_sb[:, :, cols], ACT.Square)
-            pairs = held.tile([P, 2, NH], F32, name=f"pairs{half}")
-            nc.vector.tensor_tensor(pairs[:], squares[:, 0:2, :], squares[:, 2:4, :], ALU.add)
-            total = held.tile([P, NH], F32, name=f"total{half}")
-            nc.vector.tensor_tensor(total[:], pairs[:, 0, :], pairs[:, 1, :], ALU.add)
-            mean_ps = psum_norm.tile([P, NH], F32, name=f"mean_ps{half}")
-            nc.tensor.matmul(mean_ps[:], averager[:], total[:], start=True, stop=True)
-            nc.scalar.activation(r[:, cols], mean_ps[:], ACT.Abs_reciprocal_sqrt, bias=eps[:], scale=1.0)
+        xg = [held.tile([P, N], BF16, name=f"xg{cb}") for cb in range(CB)]
+        squares = [held.tile([P, N], F32, name=f"squares{cb}") for cb in range(CB)]
+        for cb in range(CB):
+            nc.vector.tensor_scalar_mul(xg[cb][:], x_sb[cb][:], gain[:, cb : cb + 1])
+            nc.scalar.activation(squares[cb][:], x_sb[cb][:], ACT.Square)
 
-        u = held.tile([P, FB, N], BF16, name="u")
-        for cols in halves:
-            r_for_pair = r[:, cols].unsqueeze(1).to_broadcast([P, PAIR, NH])
-            for q in range(FQ):
-                u_ps = psum_u.tile([P, PAIR, NH], F32, name="u_ps")
+        first_two = held.tile([P, N], F32, name="first_two")
+        nc.vector.tensor_tensor(first_two[:], squares[0][:], squares[1][:], ALU.add)
+        last_two = held.tile([P, N], F32, name="last_two")
+        nc.vector.tensor_tensor(last_two[:], squares[2][:], squares[3][:], ALU.add)
+        total = held.tile([P, N], F32, name="total")
+        nc.vector.tensor_tensor(total[:], first_two[:], last_two[:], ALU.add)
+        mean_ps = psum_norm.tile([P, N], F32, name="mean_ps")
+        nc.tensor.matmul(mean_ps[:], averager[:], total[:], start=True, stop=True)
+        r = held.tile([P, N], F32, name="r")
+        nc.scalar.activation(r[:], mean_ps[:], ACT.Abs_reciprocal_sqrt, bias=eps[:], scale=1.0)
+
+        u = [held.tile([P, N], BF16, name=f"u{fb}") for fb in range(FB)]
+        for q in range(FQ):
+            u_ps = [psum_sums.tile([P, N], F32, name="sums") for i in range(PAIR)]
+            for cb in range(CB):
                 for i in range(PAIR):
-                    for cb in range(CB):
-                        nc.tensor.matmul(
-                            u_ps[:, i, :],
-                            w1_sb[q][:, cb, i * P : (i + 1) * P],
-                            xg[:, cb, cols],
-                            start=(cb == 0),
-                            stop=(cb == CB - 1),
-                        )
-                scaled = scaled_ring.tile([P, PAIR, NH], F32, name="scaled")
-                nc.vector.tensor_tensor(scaled[:], u_ps[:], r_for_pair, ALU.mult)
-                nc.scalar.activation(u[:, q * PAIR : (q + 1) * PAIR, cols], scaled[:], ACT.Gelu)
+                    nc.tensor.matmul(
+                        u_ps[i][:],
+                        w1_sb[q][:, cb, i * P : (i + 1) * P],
+                        xg[cb][:],
+                        start=(cb == 0),
+                        stop=(cb == CB - 1),
+                    )
+            for i in range(PAIR):
+                scaled = scaled_ring.tile([P, N], F32, name="scaled")
+                nc.vector.tensor_tensor(scaled[:], u_ps[i][:], r[:], ALU.mult)
+                nc.scalar.activation(u[q * PAIR + i][:], scaled[:], ACT.Gelu)
 
         for cb in range(CB):
-            y_ps = psum_u.tile([P, N], F32, name="y_ps", tag="u_ps")
+            y_ps = psum_sums.tile([P, N], F32, name="sums")
             for fb in range(FB):
                 nc.tensor.matmul(
                     y_ps[:],
                     w2_sb[fb // (FB // 2)][:, fb % (FB // 2), cb * P : (cb + 1) * P],
-                    u[:, fb, :],
+                    u[fb][:],
                     start=(fb == 0),
                     stop=(fb == FB - 1),
                 )
             y = ring.tile([P, N], F32, name="y")
             nc.scalar.copy(y[:], y_ps[:])
-            nc.vector.tensor_tensor(window[cb][:].indirect(offsets[:]), y[:], x_sb[:, cb, :], ALU.add)
+            nc.vector.tensor_tensor(window[cb][:].indirect(offsets[:]), y[:], x_sb[cb][:], ALU.add)
             nc.sync.dma_start(out[cb * P : (cb + 1) * P, :], window[cb][:])

@@ -38,9 +38,8 @@ def tile_synthetictransformer_kernel(tc, base, x, norm_w, w1, w2, offs, out):
             nc.scalar.dma_start(gain[:], norm_w.rearrange("(cb p) o -> p (cb o)", p=P))
         nc.sync.dma_start(x_sb[0][:], x[0:P, :])
         nc.sync.dma_start(w1_sb[0][:], w1_pieces[0])
-        nc.scalar.dma_start(x_sb[1][:], x[P : 2 * P, :])
-        nc.sync.dma_start(x_sb[2][:], x[2 * P : 3 * P, :])
-        nc.scalar.dma_start(x_sb[3][:], x[3 * P : 4 * P, :])
+        for cb in range(1, CB):
+            nc.sync.dma_start(x_sb[cb][:], x[cb * P : (cb + 1) * P, :])
         for q in range(1, FQ):
             nc.sync.dma_start(w1_sb[q][:], w1_pieces[q])
 

@@ -13,9 +13,8 @@ C, F, S, N = 512, 2048, 2048, 512
 CB = C // P
 FB = F // P
 EPS = 1e-6
-PAIR = 2
-FQ = FB // PAIR
-FW = F // FQ
+GROUPS = [4, 2, 2, 2, 2, 2, 2]
+assert sum(GROUPS) == FB
 WARM_UP = 4
 
 FLOPS = 2 * C * F * N * 2
@@ -27,21 +26,27 @@ def tile_synthetictransformer_kernel(tc, base, x, norm_w, w1, w2, offs, out):
         held = ctx.enter_context(tc.tile_pool(name="held", bufs=1))
         ring = ctx.enter_context(tc.tile_pool(name="ring", bufs=2))
         scaled_ring = ctx.enter_context(tc.tile_pool(name="scaled_ring", bufs=8))
-        psum_sums = ctx.enter_context(tc.psum_pool(name="psum_sums", bufs=6))
+        psum_sums = ctx.enter_context(tc.psum_pool(name="psum_sums", bufs=7))
         psum_norm = ctx.enter_context(tc.psum_pool(name="psum_norm", bufs=1))
 
         x_sb = [held.tile([P, N], F32, name=f"x{cb}") for cb in range(CB)]
-        w1_sb = [held.tile([P, CB, FW], BF16, name=f"w1_{q}") for q in range(FQ)]
-        w1_pieces = [w1[:, q * FW : (q + 1) * FW].rearrange("(cb p) f -> p cb f", p=P) for q in range(FQ)]
         gain = held.tile([P, CB], F32, name="gain")
+        first_block = [sum(GROUPS[:g]) for g in range(len(GROUPS))]
+        w1_sb = [held.tile([P, CB, width * P], BF16, name=f"w1_{g}") for g, width in enumerate(GROUPS)]
+        w1_pieces = [
+            w1[:, first_block[g] * P : (first_block[g] + width) * P].rearrange("(cb p) f -> p cb f", p=P)
+            for g, width in enumerate(GROUPS)
+        ]
         with nc.allow_non_contiguous_dma(reason="512 single values"):
             nc.scalar.dma_start(gain[:], norm_w.rearrange("(cb p) o -> p (cb o)", p=P))
         nc.sync.dma_start(x_sb[0][:], x[0:P, :])
-        nc.sync.dma_start(w1_sb[0][:], w1_pieces[0])
-        for cb in range(1, CB):
-            nc.sync.dma_start(x_sb[cb][:], x[cb * P : (cb + 1) * P, :])
-        for q in range(1, FQ):
-            nc.sync.dma_start(w1_sb[q][:], w1_pieces[q])
+        nc.sync.dma_start(w1_sb[0][:, 0:2, :], w1_pieces[0][:, 0:2, :])
+        nc.sync.dma_start(x_sb[1][:], x[P : 2 * P, :])
+        nc.sync.dma_start(x_sb[2][:], x[2 * P : 3 * P, :])
+        nc.sync.dma_start(w1_sb[0][:, 2:4, :], w1_pieces[0][:, 2:4, :])
+        nc.sync.dma_start(x_sb[3][:], x[3 * P : 4 * P, :])
+        for g in range(1, len(GROUPS)):
+            nc.sync.dma_start(w1_sb[g][:], w1_pieces[g])
 
         offsets = held.tile([P, N // 16], U16, name="offsets")
         nc.sync.dma_start(offsets[:], offs)
@@ -67,7 +72,7 @@ def tile_synthetictransformer_kernel(tc, base, x, norm_w, w1, w2, offs, out):
         first_call = held.tile([P, 1], F32, name="first_call")
         nc.scalar.activation(first_call[:], eps[:], ACT.Abs_reciprocal_sqrt)
 
-        idle_ps = psum_norm.tile([P, N], F32, name="idle_ps")
+        idle_ps = psum_norm.tile([P, N], F32, name="idle_ps", tag="norm")
         for i in range(WARM_UP):
             nc.tensor.matmul(idle_ps[:], zeros[:, 0:P], zeros[:], start=True, stop=True)
 
@@ -83,27 +88,27 @@ def tile_synthetictransformer_kernel(tc, base, x, norm_w, w1, w2, offs, out):
         nc.vector.tensor_tensor(last_two[:], squares[2][:], squares[3][:], ALU.add)
         total = held.tile([P, N], F32, name="total")
         nc.vector.tensor_tensor(total[:], first_two[:], last_two[:], ALU.add)
-        mean_ps = psum_norm.tile([P, N], F32, name="mean_ps")
+        mean_ps = psum_norm.tile([P, N], F32, name="mean_ps", tag="norm")
         nc.tensor.matmul(mean_ps[:], averager[:], total[:], start=True, stop=True)
         r = held.tile([P, N], F32, name="r")
         nc.scalar.activation(r[:], mean_ps[:], ACT.Abs_reciprocal_sqrt, bias=eps[:], scale=1.0)
 
         u = [held.tile([P, N], BF16, name=f"u{fb}") for fb in range(FB)]
-        for q in range(FQ):
-            u_ps = [psum_sums.tile([P, N], F32, name="sums") for i in range(PAIR)]
+        for g, width in enumerate(GROUPS):
+            u_ps = [psum_sums.tile([P, N], F32, name="sums") for i in range(width)]
             for cb in range(CB):
-                for i in range(PAIR):
+                for i in range(width):
                     nc.tensor.matmul(
                         u_ps[i][:],
-                        w1_sb[q][:, cb, i * P : (i + 1) * P],
+                        w1_sb[g][:, cb, i * P : (i + 1) * P],
                         xg[cb][:],
                         start=(cb == 0),
                         stop=(cb == CB - 1),
                     )
-            for i in range(PAIR):
+            for i in range(width):
                 scaled = scaled_ring.tile([P, N], F32, name="scaled")
                 nc.vector.tensor_tensor(scaled[:], u_ps[i][:], r[:], ALU.mult)
-                nc.scalar.activation(u[q * PAIR + i][:], scaled[:], ACT.Gelu)
+                nc.scalar.activation(u[first_block[g] + i][:], scaled[:], ACT.Gelu)
 
         for cb in range(CB):
             y_ps = psum_sums.tile([P, N], F32, name="sums")

@@ -15,7 +15,6 @@ FB = F // P
 EPS = 1e-6
 GROUPS = [4, 2, 2, 2, 2, 2, 2]
 assert sum(GROUPS) == FB
-WARM_UP = 4
 
 FLOPS = 2 * C * F * N * 2
 
@@ -62,8 +61,6 @@ def tile_synthetictransformer_kernel(tc, base, x, norm_w, w1, w2, offs, out):
         for cb in range(CB):
             nc.sync.dma_start(window[cb][:], base[cb * P : (cb + 1) * P, :])
 
-        zeros = held.tile([P, N], BF16, name="zeros")
-        nc.vector.memset(zeros[:], 0.0)
         averager = held.tile([P, P], F32, name="averager")
         nc.vector.memset(averager[:], 1.0 / C)
         eps = held.tile([P, 1], F32, name="eps")
@@ -71,10 +68,6 @@ def tile_synthetictransformer_kernel(tc, base, x, norm_w, w1, w2, offs, out):
 
         first_call = held.tile([P, 1], F32, name="first_call")
         nc.scalar.activation(first_call[:], eps[:], ACT.Abs_reciprocal_sqrt)
-
-        idle_ps = psum_norm.tile([P, N], F32, name="idle_ps", tag="norm")
-        for i in range(WARM_UP):
-            nc.tensor.matmul(idle_ps[:], zeros[:, 0:P], zeros[:], start=True, stop=True)
 
         xg = [held.tile([P, N], BF16, name=f"xg{cb}") for cb in range(CB)]
         squares = [held.tile([P, N], F32, name=f"squares{cb}") for cb in range(CB)]
@@ -88,7 +81,7 @@ def tile_synthetictransformer_kernel(tc, base, x, norm_w, w1, w2, offs, out):
         nc.vector.tensor_tensor(last_two[:], squares[2][:], squares[3][:], ALU.add)
         total = held.tile([P, N], F32, name="total")
         nc.vector.tensor_tensor(total[:], first_two[:], last_two[:], ALU.add)
-        mean_ps = psum_norm.tile([P, N], F32, name="mean_ps", tag="norm")
+        mean_ps = psum_norm.tile([P, N], F32, name="mean_ps")
         nc.tensor.matmul(mean_ps[:], averager[:], total[:], start=True, stop=True)
         r = held.tile([P, N], F32, name="r")
         nc.scalar.activation(r[:], mean_ps[:], ACT.Abs_reciprocal_sqrt, bias=eps[:], scale=1.0)
@@ -111,16 +104,20 @@ def tile_synthetictransformer_kernel(tc, base, x, norm_w, w1, w2, offs, out):
                 nc.scalar.activation(u[first_block[g] + i][:], scaled[:], ACT.Gelu)
 
         for cb in range(CB):
-            y_ps = psum_sums.tile([P, N], F32, name="sums")
-            for fb in range(FB):
-                nc.tensor.matmul(
-                    y_ps[:],
-                    w2_sb[fb // (FB // 2)][:, fb % (FB // 2), cb * P : (cb + 1) * P],
-                    u[fb][:],
-                    start=(fb == 0),
-                    stop=(fb == FB - 1),
-                )
             y = ring.tile([P, N], F32, name="y")
-            nc.scalar.copy(y[:], y_ps[:])
+            pieces = 2 if cb == CB - 1 else 1
+            width = N // pieces
+            for piece in range(pieces):
+                cols = slice(piece * width, (piece + 1) * width)
+                y_ps = psum_sums.tile([P, N], F32, name="sums")
+                for fb in range(FB):
+                    nc.tensor.matmul(
+                        y_ps[:, 0:width],
+                        w2_sb[fb // (FB // 2)][:, fb % (FB // 2), cb * P : (cb + 1) * P],
+                        u[fb][:, cols],
+                        start=(fb == 0),
+                        stop=(fb == FB - 1),
+                    )
+                nc.scalar.copy(y[:, cols], y_ps[:, 0:width])
             nc.vector.tensor_tensor(window[cb][:].indirect(offsets[:]), y[:], x_sb[cb][:], ALU.add)
             nc.sync.dma_start(out[cb * P : (cb + 1) * P, :], window[cb][:])

@@ -33,17 +33,17 @@ def tile_synthetictransformer_kernel(tc, base, x, norm_w, w1, w2, offs, out):
         first_block = [sum(GROUPS[:g]) for g in range(len(GROUPS))]
         w1_sb = [held.tile([P, CB, width * P], BF16, name=f"w1_{g}") for g, width in enumerate(GROUPS)]
         w1_pieces = [
-            w1[:, first_block[g] * P : (first_block[g] + width) * P].rearrange("(cb p) f -> p cb f", p=P)
+            w1[:, first_block[g] * P : (first_block[g] + width) * P].rearrange("(p cb) f -> p cb f", cb=CB)
             for g, width in enumerate(GROUPS)
         ]
-        with nc.allow_non_contiguous_dma(reason="512 single values"):
-            nc.scalar.dma_start(gain[:], norm_w.rearrange("(cb p) o -> p (cb o)", p=P))
-        nc.sync.dma_start(x_sb[0][:], x[0:P, :])
+        x_blocks = x.rearrange("(p cb) j -> cb p j", cb=CB)
+        nc.scalar.dma_start(gain[:], norm_w.rearrange("(p cb) o -> p (cb o)", cb=CB))
+        nc.sync.dma_start(x_sb[0][:], x_blocks[0])
         nc.sync.dma_start(w1_sb[0][:, 0:2, :], w1_pieces[0][:, 0:2, :])
-        nc.sync.dma_start(x_sb[1][:], x[P : 2 * P, :])
-        nc.sync.dma_start(x_sb[2][:], x[2 * P : 3 * P, :])
+        nc.sync.dma_start(x_sb[1][:], x_blocks[1])
+        nc.sync.dma_start(x_sb[2][:], x_blocks[2])
         nc.sync.dma_start(w1_sb[0][:, 2:4, :], w1_pieces[0][:, 2:4, :])
-        nc.sync.dma_start(x_sb[3][:], x[3 * P : 4 * P, :])
+        nc.sync.dma_start(x_sb[3][:], x_blocks[3])
         for g in range(1, len(GROUPS)):
             nc.sync.dma_start(w1_sb[g][:], w1_pieces[g])
 
@@ -51,6 +51,7 @@ def tile_synthetictransformer_kernel(tc, base, x, norm_w, w1, w2, offs, out):
         nc.sync.dma_start(offsets[:], offs)
 
         w2_sb = [held.tile([P, FB // 2, C], BF16, name=f"w2_{part}") for part in range(2)]
+        w2_blocks = [w2_sb[part][:].rearrange("k fb (m cb) -> k fb cb m", cb=CB) for part in range(2)]
         for part in range(2):
             nc.sync.dma_start(
                 w2_sb[part][:],
@@ -58,8 +59,10 @@ def tile_synthetictransformer_kernel(tc, base, x, norm_w, w1, w2, offs, out):
             )
 
         window = [held.tile([P, S], F32, name=f"window{cb}") for cb in range(CB)]
+        base_blocks = base.rearrange("(p cb) s -> cb p s", cb=CB)
+        out_blocks = out.rearrange("(p cb) s -> cb p s", cb=CB)
         for cb in range(CB):
-            nc.sync.dma_start(window[cb][:], base[cb * P : (cb + 1) * P, :])
+            nc.sync.dma_start(window[cb][:], base_blocks[cb])
 
         averager = held.tile([P, P], F32, name="averager")
         nc.vector.memset(averager[:], 1.0 / C)
@@ -113,11 +116,11 @@ def tile_synthetictransformer_kernel(tc, base, x, norm_w, w1, w2, offs, out):
                 for fb in range(FB):
                     nc.tensor.matmul(
                         y_ps[:, 0:width],
-                        w2_sb[fb // (FB // 2)][:, fb % (FB // 2), cb * P : (cb + 1) * P],
+                        w2_blocks[fb // (FB // 2)][:, fb % (FB // 2), cb, :],
                         u[fb][:, cols],
                         start=(fb == 0),
                         stop=(fb == FB - 1),
                     )
                 nc.scalar.copy(y[:, cols], y_ps[:, 0:width])
             nc.vector.tensor_tensor(window[cb][:].indirect(offsets[:]), y[:], x_sb[cb][:], ALU.add)
-            nc.sync.dma_start(out[cb * P : (cb + 1) * P, :], window[cb][:])
+            nc.sync.dma_start(out_blocks[cb], window[cb][:])

@@ -42,8 +42,8 @@ def tile_synthetictransformer_kernel(tc, base, x, norm_w, w1, w2, offs, out):
         nc.sync.dma_start(w1_sb[0][:, 0:2, :], w1_pieces[0][:, 0:2, :])
         nc.sync.dma_start(x_sb[1][:], x_blocks[1])
         nc.sync.dma_start(x_sb[2][:], x_blocks[2])
-        nc.sync.dma_start(w1_sb[0][:, 2:4, :], w1_pieces[0][:, 2:4, :])
         nc.sync.dma_start(x_sb[3][:], x_blocks[3])
+        nc.sync.dma_start(w1_sb[0][:, 2:4, :], w1_pieces[0][:, 2:4, :])
         for g in range(1, len(GROUPS)):
             nc.sync.dma_start(w1_sb[g][:], w1_pieces[g])
 
@@ -64,7 +64,7 @@ def tile_synthetictransformer_kernel(tc, base, x, norm_w, w1, w2, offs, out):
         for cb in range(CB):
             nc.sync.dma_start(window[cb][:], base_blocks[cb])
 
-        averager = held.tile([P, P], F32, name="averager")
+        averager = held.tile([P, P], BF16, name="averager")
         nc.vector.memset(averager[:], 1.0 / C)
         eps = held.tile([P, 1], F32, name="eps")
         nc.vector.memset(eps[:], EPS)
@@ -74,18 +74,26 @@ def tile_synthetictransformer_kernel(tc, base, x, norm_w, w1, w2, offs, out):
 
         xg = [held.tile([P, N], BF16, name=f"xg{cb}") for cb in range(CB)]
         squares = [held.tile([P, N], F32, name=f"squares{cb}") for cb in range(CB)]
+        running = [squares[0]] + [held.tile([P, N], F32, name=f"running{cb}") for cb in range(1, CB)]
         for cb in range(CB):
             nc.vector.tensor_scalar_mul(xg[cb][:], x_sb[cb][:], gain[:, cb : cb + 1])
             nc.scalar.activation(squares[cb][:], x_sb[cb][:], ACT.Square)
+        for cb in range(1, CB):
+            nc.vector.tensor_tensor(running[cb][:], running[cb - 1][:], squares[cb][:], ALU.add)
+        total = running[CB - 1]
 
-        first_two = held.tile([P, N], F32, name="first_two")
-        nc.vector.tensor_tensor(first_two[:], squares[0][:], squares[1][:], ALU.add)
-        last_two = held.tile([P, N], F32, name="last_two")
-        nc.vector.tensor_tensor(last_two[:], squares[2][:], squares[3][:], ALU.add)
-        total = held.tile([P, N], F32, name="total")
-        nc.vector.tensor_tensor(total[:], first_two[:], last_two[:], ALU.add)
+        top = held.tile([P, N], BF16, name="top")
+        nc.vector.tensor_copy(top[:], total[:])
+        below_top = held.tile([P, N], F32, name="below_top")
+        nc.vector.tensor_tensor(below_top[:], total[:], top[:], ALU.subtract)
+        middle = held.tile([P, N], BF16, name="middle")
+        nc.vector.tensor_copy(middle[:], below_top[:])
+        rest = held.tile([P, N], BF16, name="rest")
+        nc.vector.tensor_tensor(rest[:], below_top[:], middle[:], ALU.subtract)
         mean_ps = psum_norm.tile([P, N], F32, name="mean_ps")
-        nc.tensor.matmul(mean_ps[:], averager[:], total[:], start=True, stop=True)
+        parts = (top, middle, rest)
+        for i, part in enumerate(parts):
+            nc.tensor.matmul(mean_ps[:], averager[:], part[:], start=(i == 0), stop=(i == len(parts) - 1))
         r = held.tile([P, N], F32, name="r")
         nc.scalar.activation(r[:], mean_ps[:], ACT.Abs_reciprocal_sqrt, bias=eps[:], scale=1.0)
 

@@ -13,8 +13,11 @@ C, F, S, N = 512, 2048, 2048, 512
 CB = C // P
 FB = F // P
 EPS = 1e-6
-GROUPS = [4, 2, 2, 2, 2, 2, 2]
+GROUPS = [4] + [1] * 12
 assert sum(GROUPS) == FB
+W1_BLOCKS = GROUPS[0]
+
+LAST_TOKENS = 64
 
 FLOPS = 2 * C * F * N * 2
 
@@ -31,10 +34,10 @@ def tile_synthetictransformer_kernel(tc, base, x, norm_w, w1, w2, offs, out):
         x_sb = [held.tile([P, N], F32, name=f"x{cb}") for cb in range(CB)]
         gain = held.tile([P, CB], F32, name="gain")
         first_block = [sum(GROUPS[:g]) for g in range(len(GROUPS))]
-        w1_sb = [held.tile([P, CB, width * P], BF16, name=f"w1_{g}") for g, width in enumerate(GROUPS)]
+        w1_sb = [held.tile([P, CB, W1_BLOCKS * P], BF16, name=f"w1_{piece}") for piece in range(FB // W1_BLOCKS)]
         w1_pieces = [
-            w1[:, first_block[g] * P : (first_block[g] + width) * P].rearrange("(p cb) f -> p cb f", cb=CB)
-            for g, width in enumerate(GROUPS)
+            w1[:, piece * W1_BLOCKS * P : (piece + 1) * W1_BLOCKS * P].rearrange("(p cb) f -> p cb f", cb=CB)
+            for piece in range(FB // W1_BLOCKS)
         ]
         x_blocks = x.rearrange("(p cb) j -> cb p j", cb=CB)
         nc.scalar.dma_start(gain[:], norm_w.rearrange("(p cb) o -> p (cb o)", cb=CB))
@@ -44,8 +47,8 @@ def tile_synthetictransformer_kernel(tc, base, x, norm_w, w1, w2, offs, out):
         nc.sync.dma_start(x_sb[2][:], x_blocks[2])
         nc.sync.dma_start(x_sb[3][:], x_blocks[3])
         nc.sync.dma_start(w1_sb[0][:, 2:4, :], w1_pieces[0][:, 2:4, :])
-        for g in range(1, len(GROUPS)):
-            nc.sync.dma_start(w1_sb[g][:], w1_pieces[g])
+        for piece in range(1, FB // W1_BLOCKS):
+            nc.sync.dma_start(w1_sb[piece][:], w1_pieces[piece])
 
         offsets = held.tile([P, N // 16], U16, name="offsets")
         nc.sync.dma_start(offsets[:], offs)
@@ -102,9 +105,10 @@ def tile_synthetictransformer_kernel(tc, base, x, norm_w, w1, w2, offs, out):
             u_ps = [psum_sums.tile([P, N], F32, name="sums") for i in range(width)]
             for cb in range(CB):
                 for i in range(width):
+                    piece, column = divmod((first_block[g] + i) * P, W1_BLOCKS * P)
                     nc.tensor.matmul(
                         u_ps[i][:],
-                        w1_sb[g][:, cb, i * P : (i + 1) * P],
+                        w1_sb[piece][:, cb, column : column + P],
                         xg[cb][:],
                         start=(cb == 0),
                         stop=(cb == CB - 1),
@@ -116,19 +120,18 @@ def tile_synthetictransformer_kernel(tc, base, x, norm_w, w1, w2, offs, out):
 
         for cb in range(CB):
             y = ring.tile([P, N], F32, name="y")
-            pieces = 2 if cb == CB - 1 else 1
-            width = N // pieces
-            for piece in range(pieces):
-                cols = slice(piece * width, (piece + 1) * width)
+            spans = [(0, N - LAST_TOKENS), (N - LAST_TOKENS, N)] if cb == CB - 1 else [(0, N)]
+            for first, end in spans:
+                cols = slice(first, end)
                 y_ps = psum_sums.tile([P, N], F32, name="sums")
                 for fb in range(FB):
                     nc.tensor.matmul(
-                        y_ps[:, 0:width],
+                        y_ps[:, 0 : end - first],
                         w2_blocks[fb // (FB // 2)][:, fb % (FB // 2), cb, :],
                         u[fb][:, cols],
                         start=(fb == 0),
                         stop=(fb == FB - 1),
                     )
-                nc.scalar.copy(y[:, cols], y_ps[:, 0:width])
+                nc.scalar.copy(y[:, cols], y_ps[:, 0 : end - first])
             nc.vector.tensor_tensor(window[cb][:].indirect(offsets[:]), y[:], x_sb[cb][:], ALU.add)
             nc.sync.dma_start(out_blocks[cb], window[cb][:])

@@ -1,18 +1,23 @@
 from contextlib import ExitStack
 
 import concourse.mybir as mybir
+from concourse.masks import make_identity
 
 F32 = mybir.dt.float32
 BF16 = mybir.dt.bfloat16
 U16 = mybir.dt.uint16
 ACT = mybir.ActivationFunctionType
 ALU = mybir.AluOpType
+AXIS = mybir.AxisListType
 
 P = 128
 C, F, S, N = 512, 2048, 2048, 512
 CB = C // P
 FB = F // P
 EPS = 1e-6
+Q = 32
+NQ = N // Q
+SPANS = [slice(0, N // 2), slice(N // 2, N)]
 GROUPS = [4] + [1] * 12
 assert sum(GROUPS) == FB
 W1_BLOCKS = GROUPS[0]
@@ -28,8 +33,7 @@ def tile_synthetictransformer_kernel(tc, base, x, norm_w, w1, w2, offs, out):
         held = ctx.enter_context(tc.tile_pool(name="held", bufs=1))
         ring = ctx.enter_context(tc.tile_pool(name="ring", bufs=2))
         scaled_ring = ctx.enter_context(tc.tile_pool(name="scaled_ring", bufs=8))
-        psum_sums = ctx.enter_context(tc.psum_pool(name="psum_sums", bufs=7))
-        psum_norm = ctx.enter_context(tc.psum_pool(name="psum_norm", bufs=1))
+        psum_sums = ctx.enter_context(tc.psum_pool(name="psum_sums", bufs=8))
 
         x_sb = [held.tile([P, N], F32, name=f"x{cb}") for cb in range(CB)]
         gain = held.tile([P, CB], F32, name="gain")
@@ -67,8 +71,16 @@ def tile_synthetictransformer_kernel(tc, base, x, norm_w, w1, w2, offs, out):
         for cb in range(CB):
             nc.sync.dma_start(window[cb][:], base_blocks[cb])
 
-        averager = held.tile([P, P], BF16, name="averager")
-        nc.vector.memset(averager[:], 1.0 / C)
+        identity = held.tile([P, P], F32, name="identity")
+        make_identity(nc, identity[:])
+        overlaid = held.tile([P, Q], F32, name="overlaid")
+        nc.vector.tensor_reduce(overlaid[:], identity[:].rearrange("k (band i) -> k i band", i=Q), AXIS.X, ALU.add)
+        gatherer = held.tile([P, P], F32, name="gatherer")
+        nc.vector.tensor_scalar_mul(
+            gatherer[:].rearrange("k (band i) -> k band i", i=Q),
+            overlaid[:].unsqueeze(1).to_broadcast([P, P // Q, Q]),
+            1.0 / C,
+        )
         eps = held.tile([P, 1], F32, name="eps")
         nc.vector.memset(eps[:], EPS)
 
@@ -77,34 +89,34 @@ def tile_synthetictransformer_kernel(tc, base, x, norm_w, w1, w2, offs, out):
 
         xg = [held.tile([P, N], BF16, name=f"xg{cb}") for cb in range(CB)]
         squares = [held.tile([P, N], F32, name=f"squares{cb}") for cb in range(CB)]
-        running = [squares[0]] + [held.tile([P, N], F32, name=f"running{cb}") for cb in range(1, CB)]
+        running = [squares[0]] + [held.tile([P, N], F32, name=f"running{cb}", align_bytes=64) for cb in range(1, CB)]
         for cb in range(CB):
             nc.vector.tensor_scalar_mul(xg[cb][:], x_sb[cb][:], gain[:, cb : cb + 1])
-            nc.scalar.activation(squares[cb][:], x_sb[cb][:], ACT.Square)
-        for cb in range(1, CB):
-            nc.vector.tensor_tensor(running[cb][:], running[cb - 1][:], squares[cb][:], ALU.add)
+            for span in SPANS:
+                nc.scalar.activation(squares[cb][:, span], x_sb[cb][:, span], ACT.Square)
+                if cb > 0:
+                    nc.vector.tensor_tensor(
+                        running[cb][:, span], running[cb - 1][:, span], squares[cb][:, span], ALU.add
+                    )
         total = running[CB - 1]
 
-        top = held.tile([P, N], BF16, name="top")
-        nc.vector.tensor_copy(top[:], total[:])
-        below_top = held.tile([P, N], F32, name="below_top")
-        nc.vector.tensor_tensor(below_top[:], total[:], top[:], ALU.subtract)
-        middle = held.tile([P, N], BF16, name="middle")
-        nc.vector.tensor_copy(middle[:], below_top[:])
-        rest = held.tile([P, N], BF16, name="rest")
-        nc.vector.tensor_tensor(rest[:], below_top[:], middle[:], ALU.subtract)
-        mean_ps = psum_norm.tile([P, N], F32, name="mean_ps")
-        parts = (top, middle, rest)
-        for i, part in enumerate(parts):
-            nc.tensor.matmul(mean_ps[:], averager[:], part[:], start=(i == 0), stop=(i == len(parts) - 1))
-        r = held.tile([P, N], F32, name="r")
-        nc.scalar.activation(r[:], mean_ps[:], ACT.Abs_reciprocal_sqrt, bias=eps[:], scale=1.0)
+        turned = held.tile([P, N], F32, name="turned", align_bytes=64)
+        part = held.tile([P, NQ], F32, name="part")
+        for span in SPANS:
+            nc.vector.transpose(turned[:, span], total[:, span])
+            nc.vector.tensor_reduce(
+                part[:, span.start // Q : span.stop // Q],
+                turned[:, span].rearrange("p (b k) -> p b k", k=Q),
+                AXIS.X,
+                ALU.add,
+            )
 
         u = [held.tile([P, N], BF16, name=f"u{fb}") for fb in range(FB)]
-        for g, width in enumerate(GROUPS):
-            u_ps = [psum_sums.tile([P, N], F32, name="sums") for i in range(width)]
+
+        def sums_of_group(g):
+            u_ps = [psum_sums.tile([P, N], F32, name="sums") for i in range(GROUPS[g])]
             for cb in range(CB):
-                for i in range(width):
+                for i in range(GROUPS[g]):
                     piece, column = divmod((first_block[g] + i) * P, W1_BLOCKS * P)
                     nc.tensor.matmul(
                         u_ps[i][:],
@@ -113,10 +125,34 @@ def tile_synthetictransformer_kernel(tc, base, x, norm_w, w1, w2, offs, out):
                         start=(cb == 0),
                         stop=(cb == CB - 1),
                     )
-            for i in range(width):
+            return u_ps
+
+        def gelu_of_group(g, u_ps):
+            for i in range(GROUPS[g]):
                 scaled = scaled_ring.tile([P, N], F32, name="scaled")
                 nc.vector.tensor_tensor(scaled[:], u_ps[i][:], r[:], ALU.mult)
                 nc.scalar.activation(u[first_block[g] + i][:], scaled[:], ACT.Gelu)
+
+        first_sums = sums_of_group(0)
+
+        mean_ps = psum_sums.tile([P, N], F32, name="sums")
+        nc.tensor.matmul(mean_ps[:, 0:NQ], gatherer[:], part[:], start=True, stop=True)
+        root = held.tile([P, N], F32, name="root", align_bytes=64)
+        r = held.tile([P, N], F32, name="r", align_bytes=64)
+        for span in SPANS:
+            mean = mean_ps[:, span.start // Q : span.stop // Q]
+            nc.scalar.activation(
+                root[:, span].rearrange("p (b k) -> p b k", k=Q),
+                mean.unsqueeze(2).to_broadcast([P, NQ // len(SPANS), Q]),
+                ACT.Abs_reciprocal_sqrt,
+                bias=eps[:],
+                scale=1.0,
+            )
+            nc.vector.transpose(r[:, span], root[:, span])
+
+        gelu_of_group(0, first_sums)
+        for g in range(1, len(GROUPS)):
+            gelu_of_group(g, sums_of_group(g))
 
         for cb in range(CB):
             y = ring.tile([P, N], F32, name="y")

@@ -133,7 +133,7 @@ def tile_synthetictransformer_kernel(tc, base, x, norm_w, w1, w2, offs, out):
                 nc.vector.tensor_tensor(scaled[:], u_ps[i][:], r[:], ALU.mult)
                 nc.scalar.activation(u[first_block[g] + i][:], scaled[:], ACT.Gelu)
 
-        first_sums = sums_of_group(0)
+        before_r = [sums_of_group(g) for g in (0, 1)]
 
         mean_ps = psum_sums.tile([P, N], F32, name="sums")
         nc.tensor.matmul(mean_ps[:, 0:NQ], gatherer[:], part[:], start=True, stop=True)
@@ -150,8 +150,9 @@ def tile_synthetictransformer_kernel(tc, base, x, norm_w, w1, w2, offs, out):
             )
             nc.vector.transpose(r[:, span], root[:, span])
 
-        gelu_of_group(0, first_sums)
-        for g in range(1, len(GROUPS)):
+        for g, u_ps in enumerate(before_r):
+            gelu_of_group(g, u_ps)
+        for g in range(len(before_r), len(GROUPS)):
             gelu_of_group(g, sums_of_group(g))
 
         for cb in range(CB):

@@ -18,9 +18,11 @@ EPS = 1e-6
 Q = 32
 NQ = N // Q
 SPANS = [slice(0, N // 2), slice(N // 2, N)]
-GROUPS = [4] + [1] * 12
-assert sum(GROUPS) == FB
-W1_BLOCKS = GROUPS[0]
+WHOLE = slice(0, N)
+FIRST_BLOCKS = 4
+BLOCKS_BY_SPANS = 2
+BLOCKS_BEFORE_MEAN = 6
+W1_BLOCKS = FIRST_BLOCKS
 
 LAST_TOKENS = 64
 
@@ -37,7 +39,6 @@ def tile_synthetictransformer_kernel(tc, base, x, norm_w, w1, w2, offs, out):
 
         x_sb = [held.tile([P, N], F32, name=f"x{cb}") for cb in range(CB)]
         gain = held.tile([P, CB], F32, name="gain")
-        first_block = [sum(GROUPS[:g]) for g in range(len(GROUPS))]
         w1_sb = [held.tile([P, CB, W1_BLOCKS * P], BF16, name=f"w1_{piece}") for piece in range(FB // W1_BLOCKS)]
         w1_pieces = [
             w1[:, piece * W1_BLOCKS * P : (piece + 1) * W1_BLOCKS * P].rearrange("(p cb) f -> p cb f", cb=CB)
@@ -45,9 +46,11 @@ def tile_synthetictransformer_kernel(tc, base, x, norm_w, w1, w2, offs, out):
         ]
         x_blocks = x.rearrange("(p cb) j -> cb p j", cb=CB)
         nc.scalar.dma_start(gain[:], norm_w.rearrange("(p cb) o -> p (cb o)", cb=CB))
-        nc.sync.dma_start(x_sb[0][:], x_blocks[0])
-        nc.sync.dma_start(w1_sb[0][:, 0:2, :], w1_pieces[0][:, 0:2, :])
+        nc.sync.dma_start(x_sb[0][:, SPANS[0]], x_blocks[0][:, SPANS[0]])
+        nc.sync.dma_start(w1_sb[0][:, 0:1, :], w1_pieces[0][:, 0:1, :])
+        nc.sync.dma_start(x_sb[0][:, SPANS[1]], x_blocks[0][:, SPANS[1]])
         nc.sync.dma_start(x_sb[1][:], x_blocks[1])
+        nc.sync.dma_start(w1_sb[0][:, 1:2, :], w1_pieces[0][:, 1:2, :])
         nc.sync.dma_start(x_sb[2][:], x_blocks[2])
         nc.sync.dma_start(x_sb[3][:], x_blocks[3])
         nc.sync.dma_start(w1_sb[0][:, 2:4, :], w1_pieces[0][:, 2:4, :])
@@ -91,8 +94,8 @@ def tile_synthetictransformer_kernel(tc, base, x, norm_w, w1, w2, offs, out):
         squares = [held.tile([P, N], F32, name=f"squares{cb}") for cb in range(CB)]
         running = [squares[0]] + [held.tile([P, N], F32, name=f"running{cb}", align_bytes=64) for cb in range(1, CB)]
         for cb in range(CB):
-            nc.vector.tensor_scalar_mul(xg[cb][:], x_sb[cb][:], gain[:, cb : cb + 1])
             for span in SPANS:
+                nc.vector.tensor_scalar_mul(xg[cb][:, span], x_sb[cb][:, span], gain[:, cb : cb + 1])
                 nc.scalar.activation(squares[cb][:, span], x_sb[cb][:, span], ACT.Square)
                 if cb > 0:
                     nc.vector.tensor_tensor(
@@ -113,27 +116,33 @@ def tile_synthetictransformer_kernel(tc, base, x, norm_w, w1, w2, offs, out):
 
         u = [held.tile([P, N], BF16, name=f"u{fb}") for fb in range(FB)]
 
-        def sums_of_group(g):
-            u_ps = [psum_sums.tile([P, N], F32, name="sums") for i in range(GROUPS[g])]
+        def sums_of(runs):
+            banks = [psum_sums.tile([P, N], F32, name="sums") for run in runs]
             for cb in range(CB):
-                for i in range(GROUPS[g]):
-                    piece, column = divmod((first_block[g] + i) * P, W1_BLOCKS * P)
+                for (fb, span), bank in zip(runs, banks):
+                    piece, column = divmod(fb * P, W1_BLOCKS * P)
                     nc.tensor.matmul(
-                        u_ps[i][:],
+                        bank[:, 0 : span.stop - span.start],
                         w1_sb[piece][:, cb, column : column + P],
-                        xg[cb][:],
+                        xg[cb][:, span],
                         start=(cb == 0),
                         stop=(cb == CB - 1),
                     )
-            return u_ps
+            return banks
 
-        def gelu_of_group(g, u_ps):
-            for i in range(GROUPS[g]):
-                scaled = scaled_ring.tile([P, N], F32, name="scaled")
-                nc.vector.tensor_tensor(scaled[:], u_ps[i][:], r[:], ALU.mult)
-                nc.scalar.activation(u[first_block[g] + i][:], scaled[:], ACT.Gelu)
+        def gelu_of(fb, sums):
+            scaled = scaled_ring.tile([P, N], F32, name="scaled")
+            nc.vector.tensor_tensor(scaled[:], sums[:], r[:], ALU.mult)
+            nc.scalar.activation(u[fb][:], scaled[:], ACT.Gelu)
 
-        before_r = [sums_of_group(g) for g in (0, 1)]
+        before_r = [held.tile([P, N], F32, name=f"copied{fb}") for fb in range(BLOCKS_BY_SPANS)]
+        by_spans = [(fb, span) for span in SPANS for fb in range(BLOCKS_BY_SPANS)]
+        banks = sums_of(by_spans + [(fb, WHOLE) for fb in range(BLOCKS_BY_SPANS, FIRST_BLOCKS)])
+        for (fb, span), bank in zip(by_spans, banks):
+            nc.scalar.copy(before_r[fb][:, span], bank[:, 0 : span.stop - span.start])
+        before_r += banks[len(by_spans) :]
+        for fb in range(FIRST_BLOCKS, BLOCKS_BEFORE_MEAN):
+            before_r += sums_of([(fb, WHOLE)])
 
         mean_ps = psum_sums.tile([P, N], F32, name="sums")
         nc.tensor.matmul(mean_ps[:, 0:NQ], gatherer[:], part[:], start=True, stop=True)
@@ -150,10 +159,11 @@ def tile_synthetictransformer_kernel(tc, base, x, norm_w, w1, w2, offs, out):
             )
             nc.vector.transpose(r[:, span], root[:, span])
 
-        for g, u_ps in enumerate(before_r):
-            gelu_of_group(g, u_ps)
-        for g in range(len(before_r), len(GROUPS)):
-            gelu_of_group(g, sums_of_group(g))
+        for fb, sums in enumerate(before_r):
+            gelu_of(fb, sums)
+        for fb in range(BLOCKS_BEFORE_MEAN, FB):
+            (sums,) = sums_of([(fb, WHOLE)])
+            gelu_of(fb, sums)
 
         for cb in range(CB):
             y = ring.tile([P, N], F32, name="y")

@@ -45,7 +45,7 @@ def tile_synthetictransformer_kernel(tc, base, x, norm_w, w1, w2, offs, out):
             for piece in range(FB // W1_BLOCKS)
         ]
         x_blocks = x.rearrange("(p cb) j -> cb p j", cb=CB)
-        nc.scalar.dma_start(gain[:], norm_w.rearrange("(p cb) o -> p (cb o)", cb=CB))
+        nc.sync.dma_start(gain[:], norm_w.rearrange("(p cb) o -> p (cb o)", cb=CB))
         nc.sync.dma_start(x_sb[0][:, SPANS[0]], x_blocks[0][:, SPANS[0]])
         nc.sync.dma_start(w1_sb[0][:, 0:1, :], w1_pieces[0][:, 0:1, :])
         nc.sync.dma_start(x_sb[0][:, SPANS[1]], x_blocks[0][:, SPANS[1]])

from contextlib import ExitStack

import concourse.mybir as mybir
from concourse.masks import make_identity

F32 = mybir.dt.float32
BF16 = mybir.dt.bfloat16
U16 = mybir.dt.uint16
ACT = mybir.ActivationFunctionType
ALU = mybir.AluOpType
AXIS = mybir.AxisListType

P = 128
C, F, S, N = 512, 2048, 2048, 512
CB = C // P
FB = F // P
EPS = 1e-6
Q = 32
NQ = N // Q
SPANS = [slice(0, N // 2), slice(N // 2, N)]
WHOLE = slice(0, N)
FIRST_BLOCKS = 4
BLOCKS_BY_SPANS = 2
BLOCKS_BEFORE_MEAN = 6
W1_BLOCKS = FIRST_BLOCKS

LAST_TOKENS = 64

FLOPS = 2 * C * F * N * 2


def tile_synthetictransformer_kernel(tc, base, x, norm_w, w1, w2, offs, out):
    nc = tc.nc
    with ExitStack() as ctx:
        held = ctx.enter_context(tc.tile_pool(name="held", bufs=1))
        ring = ctx.enter_context(tc.tile_pool(name="ring", bufs=2))
        scaled_ring = ctx.enter_context(tc.tile_pool(name="scaled_ring", bufs=8))
        psum_sums = ctx.enter_context(tc.psum_pool(name="psum_sums", bufs=8))

        x_sb = [held.tile([P, N], F32, name=f"x{cb}") for cb in range(CB)]
        gain = held.tile([P, CB], F32, name="gain")
        w1_sb = [held.tile([P, CB, W1_BLOCKS * P], BF16, name=f"w1_{piece}") for piece in range(FB // W1_BLOCKS)]
        w1_pieces = [
            w1[:, piece * W1_BLOCKS * P : (piece + 1) * W1_BLOCKS * P].rearrange("(p cb) f -> p cb f", cb=CB)
            for piece in range(FB // W1_BLOCKS)
        ]
        x_blocks = x.rearrange("(p cb) j -> cb p j", cb=CB)
        nc.sync.dma_start(gain[:], norm_w.rearrange("(p cb) o -> p (cb o)", cb=CB))
        nc.sync.dma_start(x_sb[0][:, SPANS[0]], x_blocks[0][:, SPANS[0]])
        nc.sync.dma_start(w1_sb[0][:, 0:1, :], w1_pieces[0][:, 0:1, :])
        nc.sync.dma_start(x_sb[0][:, SPANS[1]], x_blocks[0][:, SPANS[1]])
        nc.sync.dma_start(x_sb[1][:], x_blocks[1])
        nc.sync.dma_start(w1_sb[0][:, 1:2, :], w1_pieces[0][:, 1:2, :])
        nc.sync.dma_start(x_sb[2][:], x_blocks[2])
        nc.sync.dma_start(x_sb[3][:], x_blocks[3])
        nc.sync.dma_start(w1_sb[0][:, 2:4, :], w1_pieces[0][:, 2:4, :])
        for piece in range(1, FB // W1_BLOCKS):
            nc.sync.dma_start(w1_sb[piece][:], w1_pieces[piece])

        offsets = held.tile([P, N // 16], U16, name="offsets")
        nc.sync.dma_start(offsets[:], offs)

        w2_sb = [held.tile([P, FB // 2, C], BF16, name=f"w2_{part}") for part in range(2)]
        w2_blocks = [w2_sb[part][:].rearrange("k fb (m cb) -> k fb cb m", cb=CB) for part in range(2)]
        for part in range(2):
            nc.sync.dma_start(
                w2_sb[part][:],
                w2[part * (F // 2) : (part + 1) * (F // 2), :].rearrange("(fb p) c -> p fb c", p=P),
            )

        window = [held.tile([P, S], F32, name=f"window{cb}") for cb in range(CB)]
        base_blocks = base.rearrange("(p cb) s -> cb p s", cb=CB)
        out_blocks = out.rearrange("(p cb) s -> cb p s", cb=CB)
        for cb in range(CB):
            nc.sync.dma_start(window[cb][:], base_blocks[cb])

        identity = held.tile([P, P], F32, name="identity")
        make_identity(nc, identity[:])
        overlaid = held.tile([P, Q], F32, name="overlaid")
        nc.vector.tensor_reduce(overlaid[:], identity[:].rearrange("k (band i) -> k i band", i=Q), AXIS.X, ALU.add)
        gatherer = held.tile([P, P], F32, name="gatherer")
        nc.vector.tensor_scalar_mul(
            gatherer[:].rearrange("k (band i) -> k band i", i=Q),
            overlaid[:].unsqueeze(1).to_broadcast([P, P // Q, Q]),
            1.0 / C,
        )
        eps = held.tile([P, 1], F32, name="eps")
        nc.vector.memset(eps[:], EPS)

        first_call = held.tile([P, 1], F32, name="first_call")
        nc.scalar.activation(first_call[:], eps[:], ACT.Abs_reciprocal_sqrt)

        xg = [held.tile([P, N], BF16, name=f"xg{cb}") for cb in range(CB)]
        squares = [held.tile([P, N], F32, name=f"squares{cb}") for cb in range(CB)]
        running = [squares[0]] + [held.tile([P, N], F32, name=f"running{cb}", align_bytes=64) for cb in range(1, CB)]
        for cb in range(CB):
            for span in SPANS:
                nc.vector.tensor_scalar_mul(xg[cb][:, span], x_sb[cb][:, span], gain[:, cb : cb + 1])
                nc.scalar.activation(squares[cb][:, span], x_sb[cb][:, span], ACT.Square)
                if cb > 0:
                    nc.vector.tensor_tensor(
                        running[cb][:, span], running[cb - 1][:, span], squares[cb][:, span], ALU.add
                    )
        total = running[CB - 1]

        turned = held.tile([P, N], F32, name="turned", align_bytes=64)
        part = held.tile([P, NQ], F32, name="part")
        for span in SPANS:
            nc.vector.transpose(turned[:, span], total[:, span])
            nc.vector.tensor_reduce(
                part[:, span.start // Q : span.stop // Q],
                turned[:, span].rearrange("p (b k) -> p b k", k=Q),
                AXIS.X,
                ALU.add,
            )

        u = [held.tile([P, N], BF16, name=f"u{fb}") for fb in range(FB)]

        def sums_of(runs):
            banks = [psum_sums.tile([P, N], F32, name="sums") for run in runs]
            for cb in range(CB):
                for (fb, span), bank in zip(runs, banks):
                    piece, column = divmod(fb * P, W1_BLOCKS * P)
                    nc.tensor.matmul(
                        bank[:, 0 : span.stop - span.start],
                        w1_sb[piece][:, cb, column : column + P],
                        xg[cb][:, span],
                        start=(cb == 0),
                        stop=(cb == CB - 1),
                    )
            return banks

        def gelu_of(fb, sums):
            scaled = scaled_ring.tile([P, N], F32, name="scaled")
            nc.vector.tensor_tensor(scaled[:], sums[:], r[:], ALU.mult)
            nc.scalar.activation(u[fb][:], scaled[:], ACT.Gelu)

        before_r = [held.tile([P, N], F32, name=f"copied{fb}") for fb in range(BLOCKS_BY_SPANS)]
        by_spans = [(fb, span) for span in SPANS for fb in range(BLOCKS_BY_SPANS)]
        banks = sums_of(by_spans + [(fb, WHOLE) for fb in range(BLOCKS_BY_SPANS, FIRST_BLOCKS)])
        for (fb, span), bank in zip(by_spans, banks):
            nc.scalar.copy(before_r[fb][:, span], bank[:, 0 : span.stop - span.start])
        before_r += banks[len(by_spans) :]
        for fb in range(FIRST_BLOCKS, BLOCKS_BEFORE_MEAN):
            before_r += sums_of([(fb, WHOLE)])

        mean_ps = psum_sums.tile([P, N], F32, name="sums")
        nc.tensor.matmul(mean_ps[:, 0:NQ], gatherer[:], part[:], start=True, stop=True)
        root = held.tile([P, N], F32, name="root", align_bytes=64)
        r = held.tile([P, N], F32, name="r", align_bytes=64)
        for span in SPANS:
            mean = mean_ps[:, span.start // Q : span.stop // Q]
            nc.scalar.activation(
                root[:, span].rearrange("p (b k) -> p b k", k=Q),
                mean.unsqueeze(2).to_broadcast([P, NQ // len(SPANS), Q]),
                ACT.Abs_reciprocal_sqrt,
                bias=eps[:],
                scale=1.0,
            )
            nc.vector.transpose(r[:, span], root[:, span])

        for fb, sums in enumerate(before_r):
            gelu_of(fb, sums)
        for fb in range(BLOCKS_BEFORE_MEAN, FB):
            (sums,) = sums_of([(fb, WHOLE)])
            gelu_of(fb, sums)

        for cb in range(CB):
            y = ring.tile([P, N], F32, name="y")
            spans = [(0, N - LAST_TOKENS), (N - LAST_TOKENS, N)] if cb == CB - 1 else [(0, N)]
            for first, end in spans:
                cols = slice(first, end)
                y_ps = psum_sums.tile([P, N], F32, name="sums")
                for fb in range(FB):
                    nc.tensor.matmul(
                        y_ps[:, 0 : end - first],
                        w2_blocks[fb // (FB // 2)][:, fb % (FB // 2), cb, :],
                        u[fb][:, cols],
                        start=(fb == 0),
                        stop=(fb == FB - 1),
                    )
                nc.scalar.copy(y[:, cols], y_ps[:, 0 : end - first])
            nc.vector.tensor_tensor(window[cb][:].indirect(offsets[:]), y[:], x_sb[cb][:], ALU.add)
            nc.sync.dma_start(out_blocks[cb], window[cb][:])
